import numpy as np
import ml_dtypes


def mxq(x, axis, fmt="e4m3"):
    dtype, down = {"e4m3": (ml_dtypes.float8_e4m3fn, 7), "e5m2": (ml_dtypes.float8_e5m2, 14)}[fmt]
    v = np.moveaxis(np.asarray(x, np.float32).astype(ml_dtypes.bfloat16).astype(np.float64), axis, -1)
    blocks = v.reshape(v.shape[:-1] + (-1, 32))
    amax = np.abs(blocks).max(-1, keepdims=True)
    byte = np.maximum(np.where(amax > 0, np.frexp(amax)[1] - 1 + 127, 0) - down, 1)
    scale = np.exp2(byte - 127.0)
    codes = (blocks / scale).astype(np.float32).astype(dtype).astype(np.float64)
    return np.moveaxis((codes * scale).reshape(v.shape), -1, axis)


WIDE = False


def mx_kscale(k):
    if not WIDE:
        return np.ones(k)
    levels = np.array([10, -10, 5, -5, 0])
    a = np.random.permutation(np.resize(levels, k // 512 * 4)).reshape(k // 512, 4)
    idx = np.arange(k)
    return np.exp2(a[idx // 512, idx % 128 // 32])


BF16 = ml_dtypes.bfloat16


def bf(x):
    return np.asarray(x, np.float32).astype(BF16)


def f64(x):
    return np.asarray(x).astype(np.float64)


M, N, D = 8192, 512, 512


def setup_inputs():
    t = mx_kscale(D)
    q = np.random.random((M, 1))
    p = np.random.random((N, 1))
    phase = np.random.random((1, D))
    near = 1.0 + np.cos(2.0 * np.pi * (q - p.T))
    gain = 0.5 + 1.5 * np.random.random((M, 1))
    feat = 1.0 + 0.8 * np.cos(2.0 * np.pi * (p - phase))
    return {"x": bf(feat * (0.5 + np.random.random((N, D))) * t),
            "adjacency": bf(gain * near * np.random.random((M, N))),
            "W": bf(np.random.standard_normal((D, D)) * 1.5 / np.sqrt(D) / t[:, None])}


def reference(x, adjacency, W):
    a = f64(adjacency)
    deg = a.sum(axis=1)
    normalized_adj = a / deg[:, None]
    pooled = mxq(normalized_adj, 1, "e4m3") @ mxq(f64(x), 0, "e4m3")
    return np.maximum(mxq(pooled, 1, "e4m3") @ mxq(f64(W), 0, "e4m3"), 0.0)

@@ -1,0 +1,236 @@
+from contextlib import ExitStack
+
+import concourse.mybir as mybir
+from concourse.masks import make_identity
+
+BF16 = mybir.dt.bfloat16
+F32 = mybir.dt.float32
+U32 = mybir.dt.uint32
+U8 = mybir.dt.uint8
+FP8X4 = mybir.dt.float8_e4m3fn_x4
+MULT = mybir.AluOpType.mult
+ADD = mybir.AluOpType.add
+RELU = mybir.ActivationFunctionType.Relu
+
+P = 128
+PACK = 4
+GATHERERS = 8192
+K = P * PACK
+FLOPS = 2 * GATHERERS * K * K * 2
+
+LOAD_TILES = 4
+UNIT_TILES = 2
+UNIT_COLS = UNIT_TILES * P
+UNITS = GATHERERS // UNIT_COLS
+LOADS = GATHERERS // (LOAD_TILES * P)
+UNITS_PER_LOAD = LOAD_TILES // UNIT_TILES
+
+GATHER_LAG = 1
+POOL_LAG = 2
+REQUANT_LAG = 3
+PROJECT_LAG = 4
+W_STEP = 1
+
+
+def tile_egcn_pa_t_kernel(tc, x, adjacency, W, out):
+    nc = tc.nc
+    with ExitStack() as ctx:
+        keep = ctx.enter_context(tc.tile_pool(name="keep", bufs=1))
+        adj = ctx.enter_context(tc.tile_pool(name="adj", bufs=LOADS))
+        work = ctx.enter_context(tc.tile_pool(name="work", bufs=3))
+        results = ctx.enter_context(tc.tile_pool(name="results", bufs=8))
+        psum_t = ctx.enter_context(tc.psum_pool(name="psum_t", bufs=2))
+        psum_pool = ctx.enter_context(tc.psum_pool(name="psum_pool", bufs=3))
+        psum_out = ctx.enter_context(tc.psum_pool(name="psum_out", bufs=3))
+        ctx.enter_context(tc.manual_schedule())
+
+        adj_view = adjacency.rearrange("(s p n) j -> s p n j", p=P, n=LOAD_TILES)
+        out_view = out.rearrange(
+            "(s p h n) g -> s h p n g", p=P, h=UNITS_PER_LOAD, n=UNIT_TILES
+        )
+
+        x_raw = keep.tile([P, PACK, K], BF16)
+        nc.sync.dma_start(
+            out=x_raw[:].rearrange("p (u e) f -> p u (e f)", u=2, e=2),
+            in_=x.rearrange("(u p e) f -> p u (e f)", u=2, p=P, e=2),
+        )
+        w_raw = keep.tile([P, PACK, K], BF16)
+        adj_rows = []
+        for s in range(LOADS):
+            a_rows = adj.tile([P, LOAD_TILES, K], BF16)
+            nc.sync.dma_start(out=a_rows[:], in_=adj_view[s])
+            adj_rows.append(a_rows)
+            if s == 0:
+                nc.sync.dma_start(
+                    out=w_raw[:], in_=W.rearrange("(t p) g -> p t g", t=PACK, p=P)
+                )
+
+        identity = keep.tile([P, P], F32)
+        make_identity(nc, identity[:])
+
+        x_grouped = keep.tile([P, K, PACK], BF16, align_bytes=64)
+        x_codes = keep.tile([P, K], U32, align_bytes=64)
+        x_scales = keep.tile([P, K], U8, align_bytes=64)
+        nc.vector.tensor_copy(out=x_grouped[:], in_=x_raw[:].rearrange("p t f -> p f t"))
+        nc.vector.quantize_mx(
+            out=x_codes[:].bitcast(FP8X4),
+            scales=x_scales[:],
+            in_=x_grouped[:].rearrange("p f t -> p (f t)"),
+        )
+        w_grouped = keep.tile([P, K, PACK], BF16, align_bytes=64)
+        w_codes = keep.tile([P, K], U32, align_bytes=64)
+        w_scales = keep.tile([P, K], U8, align_bytes=64)
+        nc.scalar.copy(out=w_grouped[:], in_=w_raw[:].rearrange("p t g -> p g t"))
+
+        def quantise_w():
+            nc.vector.quantize_mx(
+                out=w_codes[:].bitcast(FP8X4),
+                scales=w_scales[:],
+                in_=w_grouped[:].rearrange("p g t -> p (g t)"),
+            )
+
+        norm_rows, degrees, inverses, turned = {}, {}, {}, {}
+        adj_grouped, adj_codes, adj_scales = {}, {}, {}
+        pooled_banks, pooled_grouped, pooled_codes, pooled_scales = {}, {}, {}, {}
+        out_banks = {}
+
+        def unit_rows(k, n):
+            return adj_rows[k // UNITS_PER_LOAD][:, (k % UNITS_PER_LOAD) * UNIT_TILES + n, :]
+
+        def sum_rows(k):
+            rows = work.tile([P, UNIT_TILES, K], BF16)
+            deg = work.tile([P, UNIT_TILES], F32)
+            for n in range(UNIT_TILES):
+                nc.vector.tensor_scalar(
+                    out=rows[:, n, :],
+                    in0=unit_rows(k, n),
+                    scalar1=1.0,
+                    scalar2=None,
+                    op0=MULT,
+                    op1=ADD,
+                    accum_out=deg[:, n : n + 1],
+                )
+            norm_rows[k], degrees[k] = rows, deg
+
+        def invert_sums(k):
+            inv = work.tile([P, UNIT_TILES], F32)
+            nc.vector.reciprocal(out=inv[:], in_=degrees[k][:])
+            inverses[k] = inv
+
+        def scale_rows(k):
+            for n in range(UNIT_TILES):
+                nc.vector.tensor_scalar(
+                    out=norm_rows[k][:, n, :],
+                    in0=unit_rows(k, n),
+                    scalar1=inverses[k][:, n : n + 1],
+                    scalar2=None,
+                    op0=MULT,
+                )
+
+        def transpose_rows(k):
+            words = norm_rows[k][:].bitcast(F32)
+            bank = psum_t.tile([P, UNIT_TILES, 2, P], F32)
+            for n in range(UNIT_TILES):
+                for u in range(2):
+                    nc.tensor.transpose(
+                        out=bank[:, n, u, :],
+                        in_=words[:, n, u * P : (u + 1) * P],
+                        identity=identity[:],
+                    )
+            turned[k] = bank
+
+        def gather_words(k):
+            grouped = work.tile([P, UNIT_COLS, PACK], BF16, align_bytes=64)
+            nc.vector.tensor_copy(
+                out=grouped[:].bitcast(F32).rearrange("p (n i) u -> p n i u", n=UNIT_TILES),
+                in_=turned[k][:].rearrange("p n u i -> p n i u"),
+            )
+            adj_grouped[k] = grouped
+
+        def quantise_adj(k):
+            codes = work.tile([P, UNIT_COLS], U32, align_bytes=64)
+            scales = work.tile([P, UNIT_COLS], U8, align_bytes=64)
+            nc.vector.quantize_mx(
+                out=codes[:].bitcast(FP8X4),
+                scales=scales[:],
+                in_=adj_grouped[k][:].rearrange("p c t -> p (c t)"),
+            )
+            adj_codes[k], adj_scales[k] = codes, scales
+
+        def pool_features(k):
+            for n in range(UNIT_TILES):
+                cols = slice(n * P, (n + 1) * P)
+                bank = psum_pool.tile([P, PACK, P], F32)
+                for t in range(PACK):
+                    feats = slice(t * P, (t + 1) * P)
+                    nc.tensor.matmul_mx(
+                        out=bank[:, t, :],
+                        lhsT=x_codes[:, feats].bitcast(FP8X4),
+                        lhsT_scale=x_scales[:, feats],
+                        rhs=adj_codes[k][:, cols].bitcast(FP8X4),
+                        rhs_scale=adj_scales[k][:, cols],
+                        start=True,
+                        stop=True,
+                    )
+                pooled_banks[k, n] = bank
+
+        def regroup_pooled(k):
+            grouped2 = work.tile([P, UNIT_COLS, PACK], BF16, align_bytes=64)
+            for n in range(UNIT_TILES):
+                nc.scalar.copy(
+                    out=grouped2[:, n * P : (n + 1) * P, :],
+                    in_=pooled_banks[k, n][:].rearrange("p t i -> p i t"),
+                )
+            pooled_grouped[k] = grouped2
+
+        def quantise_pooled(k):
+            codes2 = work.tile([P, UNIT_COLS], U32, align_bytes=64)
+            scales2 = work.tile([P, UNIT_COLS], U8, align_bytes=64)
+            nc.vector.quantize_mx(
+                out=codes2[:].bitcast(FP8X4),
+                scales=scales2[:],
+                in_=pooled_grouped[k][:].rearrange("p c t -> p (c t)"),
+            )
+            pooled_codes[k], pooled_scales[k] = codes2, scales2
+
+        def project(k):
+            for n in range(UNIT_TILES):
+                cols = slice(n * P, (n + 1) * P)
+                acc = psum_out.tile([P, K], F32)
+                nc.tensor.matmul_mx(
+                    out=acc[:],
+                    lhsT=pooled_codes[k][:, cols].bitcast(FP8X4),
+                    lhsT_scale=pooled_scales[k][:, cols],
+                    rhs=w_codes[:].bitcast(FP8X4),
+                    rhs_scale=w_scales[:],
+                    start=True,
+                    stop=True,
+                )
+                out_banks[k, n] = acc
+
+        def relu_and_store(k):
+            result = results.tile([P, UNIT_TILES, K], F32)
+            for n in range(UNIT_TILES):
+                nc.scalar.activation(out=result[:, n, :], in_=out_banks[k, n][:], func=RELU)
+            nc.sync.dma_start(
+                out=out_view[k // UNITS_PER_LOAD, k % UNITS_PER_LOAD], in_=result[:]
+            )
+
+        def run(stage, k):
+            if 0 <= k < UNITS:
+                stage(k)
+
+        for step in range(UNITS + PROJECT_LAG):
+            run(sum_rows, step)
+            run(pool_features, step - POOL_LAG)
+            run(gather_words, step - GATHER_LAG)
+            run(regroup_pooled, step - POOL_LAG)
+            run(invert_sums, step)
+            run(project, step - PROJECT_LAG)
+            run(quantise_pooled, step - REQUANT_LAG)
+            run(relu_and_store, step - PROJECT_LAG)
+            run(scale_rows, step)
+            run(transpose_rows, step)
+            run(quantise_adj, step - GATHER_LAG)
+            if step == W_STEP:
+                quantise_w()

@@ -10,6 +10,8 @@ U8 = mybir.dt.uint8
 FP8X4 = mybir.dt.float8_e4m3fn_x4
 MULT = mybir.AluOpType.mult
 ADD = mybir.AluOpType.add
+MAX = mybir.AluOpType.max
+AXIS_X = mybir.AxisListType.X
 RELU = mybir.ActivationFunctionType.Relu
 
 P = 128
@@ -24,12 +26,26 @@ UNIT_COLS = UNIT_TILES * P
 UNITS = GATHERERS // UNIT_COLS
 LOADS = GATHERERS // (LOAD_TILES * P)
 UNITS_PER_LOAD = LOAD_TILES // UNIT_TILES
+SUM_COLS = 64
 
-GATHER_LAG = 1
-POOL_LAG = 2
-REQUANT_LAG = 3
-PROJECT_LAG = 4
-W_STEP = 1
+GATHER_LAG = 2
+POOL_LAG = 3
+REQUANT_LAG = 4
+PROJECT_LAG = 5
+SCALAR_GATHERS = 2
+W_STEP = 4
+
+
+def tensor_sums(k, n):
+    return n == 1 or 0 < k < 3
+
+
+def vector_relu(k, n):
+    return (k % 4 == 3 and n == 1) or (k >= UNITS - 4 and n == 1)
+
+
+def vector_regroup(k, n):
+    return k == UNITS - 1 and n == 1
 
 
 def tile_egcn_pa_t_kernel(tc, x, adjacency, W, out):
@@ -37,11 +53,12 @@ def tile_egcn_pa_t_kernel(tc, x, adjacency, W, out):
     with ExitStack() as ctx:
         keep = ctx.enter_context(tc.tile_pool(name="keep", bufs=1))
         adj = ctx.enter_context(tc.tile_pool(name="adj", bufs=LOADS))
-        work = ctx.enter_context(tc.tile_pool(name="work", bufs=3))
+        work = ctx.enter_context(tc.tile_pool(name="work", bufs=6))
         results = ctx.enter_context(tc.tile_pool(name="results", bufs=8))
         psum_t = ctx.enter_context(tc.psum_pool(name="psum_t", bufs=2))
-        psum_pool = ctx.enter_context(tc.psum_pool(name="psum_pool", bufs=3))
-        psum_out = ctx.enter_context(tc.psum_pool(name="psum_out", bufs=3))
+        psum_pool = ctx.enter_context(tc.psum_pool(name="psum_pool", bufs=2))
+        psum_out = ctx.enter_context(tc.psum_pool(name="psum_out", bufs=2))
+        psum_sum = ctx.enter_context(tc.psum_pool(name="psum_sum", bufs=2))
         ctx.enter_context(tc.manual_schedule())
 
         adj_view = adjacency.rearrange("(s p n) j -> s p n j", p=P, n=LOAD_TILES)
@@ -50,37 +67,52 @@ def tile_egcn_pa_t_kernel(tc, x, adjacency, W, out):
         )
 
         x_raw = keep.tile([P, PACK, K], BF16)
-        nc.sync.dma_start(
-            out=x_raw[:].rearrange("p (u e) f -> p u (e f)", u=2, e=2),
-            in_=x.rearrange("(u p e) f -> p u (e f)", u=2, p=P, e=2),
-        )
         w_raw = keep.tile([P, PACK, K], BF16)
         adj_rows = []
         for s in range(LOADS):
             a_rows = adj.tile([P, LOAD_TILES, K], BF16)
-            nc.sync.dma_start(out=a_rows[:], in_=adj_view[s])
-            adj_rows.append(a_rows)
             if s == 0:
+                nc.sync.dma_start(out=a_rows[:, :UNIT_TILES, :], in_=adj_view[s, :, :UNIT_TILES, :])
+                nc.sync.dma_start(
+                    out=x_raw[:].rearrange("p (u e) f -> p u (e f)", u=2, e=2),
+                    in_=x.rearrange("(u p e) f -> p u (e f)", u=2, p=P, e=2),
+                )
+                nc.sync.dma_start(out=a_rows[:, UNIT_TILES:, :], in_=adj_view[s, :, UNIT_TILES:, :])
+            else:
+                nc.sync.dma_start(out=a_rows[:], in_=adj_view[s])
+            adj_rows.append(a_rows)
+            if s == 1:
                 nc.sync.dma_start(
                     out=w_raw[:], in_=W.rearrange("(t p) g -> p t g", t=PACK, p=P)
                 )
 
+        ident_bf16 = keep.tile([P, P], BF16)
+        make_identity(nc, ident_bf16[:])
         identity = keep.tile([P, P], F32)
         make_identity(nc, identity[:])
 
         x_grouped = keep.tile([P, K, PACK], BF16, align_bytes=64)
         x_codes = keep.tile([P, K], U32, align_bytes=64)
         x_scales = keep.tile([P, K], U8, align_bytes=64)
-        nc.vector.tensor_copy(out=x_grouped[:], in_=x_raw[:].rearrange("p t f -> p f t"))
-        nc.vector.quantize_mx(
-            out=x_codes[:].bitcast(FP8X4),
-            scales=x_scales[:],
-            in_=x_grouped[:].rearrange("p f t -> p (f t)"),
-        )
         w_grouped = keep.tile([P, K, PACK], BF16, align_bytes=64)
         w_codes = keep.tile([P, K], U32, align_bytes=64)
         w_scales = keep.tile([P, K], U8, align_bytes=64)
-        nc.scalar.copy(out=w_grouped[:], in_=w_raw[:].rearrange("p t g -> p g t"))
+
+        def group_x(engine_copy, first, last):
+            engine_copy(
+                out=x_grouped[:, first:last, :],
+                in_=x_raw[:, :, first:last].rearrange("p t f -> p f t"),
+            )
+
+        def quantise_x():
+            nc.vector.quantize_mx(
+                out=x_codes[:].bitcast(FP8X4),
+                scales=x_scales[:],
+                in_=x_grouped[:].rearrange("p f t -> p (f t)"),
+            )
+
+        def group_w():
+            nc.scalar.copy(out=w_grouped[:], in_=w_raw[:].rearrange("p t g -> p g t"))
 
         def quantise_w():
             nc.vector.quantize_mx(
@@ -89,27 +121,54 @@ def tile_egcn_pa_t_kernel(tc, x, adjacency, W, out):
                 in_=w_grouped[:].rearrange("p g t -> p (g t)"),
             )
 
-        norm_rows, degrees, inverses, turned = {}, {}, {}, {}
+        norm_rows, degrees, inverses, turned, folded = {}, {}, {}, {}, {}
         adj_grouped, adj_codes, adj_scales = {}, {}, {}
         pooled_banks, pooled_grouped, pooled_codes, pooled_scales = {}, {}, {}, {}
-        out_banks = {}
+        out_banks, out_rows = {}, {}
 
         def unit_rows(k, n):
             return adj_rows[k // UNITS_PER_LOAD][:, (k % UNITS_PER_LOAD) * UNIT_TILES + n, :]
 
+        def fold_rows(k):
+            whole_bank = psum_sum.tile([P, K], F32)
+            bank = whole_bank[:, : UNIT_TILES * SUM_COLS].rearrange(
+                "p (n w) -> p n w", n=UNIT_TILES
+            )
+            blocks = K // SUM_COLS
+            for n in range(UNIT_TILES):
+                if not tensor_sums(k, n):
+                    continue
+                for b in range(blocks):
+                    nc.tensor.matmul(
+                        out=bank[:, n, :],
+                        lhsT=ident_bf16[:],
+                        rhs=unit_rows(k, n)[:, b * SUM_COLS : (b + 1) * SUM_COLS],
+                        start=(b == 0),
+                        stop=(b == blocks - 1),
+                    )
+            folded[k] = bank
+
         def sum_rows(k):
             rows = work.tile([P, UNIT_TILES, K], BF16)
             deg = work.tile([P, UNIT_TILES], F32)
-            for n in range(UNIT_TILES):
-                nc.vector.tensor_scalar(
-                    out=rows[:, n, :],
-                    in0=unit_rows(k, n),
-                    scalar1=1.0,
-                    scalar2=None,
-                    op0=MULT,
-                    op1=ADD,
-                    accum_out=deg[:, n : n + 1],
-                )
+            if all(tensor_sums(k, n) for n in range(UNIT_TILES)):
+                nc.vector.tensor_reduce(out=deg[:], in_=folded[k], axis=AXIS_X, op=ADD)
+            else:
+                for n in range(UNIT_TILES):
+                    if tensor_sums(k, n):
+                        nc.vector.tensor_reduce(
+                            out=deg[:, n : n + 1], in_=folded[k][:, n, :], axis=AXIS_X, op=ADD
+                        )
+                        continue
+                    nc.vector.tensor_scalar(
+                        out=rows[:, n, :],
+                        in0=unit_rows(k, n),
+                        scalar1=1.0,
+                        scalar2=None,
+                        op0=MULT,
+                        op1=ADD,
+                        accum_out=deg[:, n : n + 1],
+                    )
             norm_rows[k], degrees[k] = rows, deg
 
         def invert_sums(k):
@@ -141,7 +200,8 @@ def tile_egcn_pa_t_kernel(tc, x, adjacency, W, out):
 
         def gather_words(k):
             grouped = work.tile([P, UNIT_COLS, PACK], BF16, align_bytes=64)
-            nc.vector.tensor_copy(
+            copy = nc.scalar.copy if k < SCALAR_GATHERS else nc.vector.tensor_copy
+            copy(
                 out=grouped[:].bitcast(F32).rearrange("p (n i) u -> p n i u", n=UNIT_TILES),
                 in_=turned[k][:].rearrange("p n u i -> p n i u"),
             )
@@ -177,10 +237,12 @@ def tile_egcn_pa_t_kernel(tc, x, adjacency, W, out):
         def regroup_pooled(k):
             grouped2 = work.tile([P, UNIT_COLS, PACK], BF16, align_bytes=64)
             for n in range(UNIT_TILES):
-                nc.scalar.copy(
-                    out=grouped2[:, n * P : (n + 1) * P, :],
-                    in_=pooled_banks[k, n][:].rearrange("p t i -> p i t"),
-                )
+                dst = grouped2[:, n * P : (n + 1) * P, :]
+                src = pooled_banks[k, n][:].rearrange("p t i -> p i t")
+                if vector_regroup(k, n):
+                    nc.vector.tensor_copy(out=dst, in_=src)
+                else:
+                    nc.scalar.copy(out=dst, in_=src)
             pooled_grouped[k] = grouped2
 
         def quantise_pooled(k):
@@ -208,29 +270,83 @@ def tile_egcn_pa_t_kernel(tc, x, adjacency, W, out):
                 )
                 out_banks[k, n] = acc
 
-        def relu_and_store(k):
+        def relu_scalar(k):
             result = results.tile([P, UNIT_TILES, K], F32)
             for n in range(UNIT_TILES):
-                nc.scalar.activation(out=result[:, n, :], in_=out_banks[k, n][:], func=RELU)
-            nc.sync.dma_start(
-                out=out_view[k // UNITS_PER_LOAD, k % UNITS_PER_LOAD], in_=result[:]
-            )
+                if not vector_relu(k, n):
+                    nc.scalar.activation(out=result[:, n, :], in_=out_banks[k, n][:], func=RELU)
+            out_rows[k] = result
+
+        def relu_vector(k):
+            for n in range(UNIT_TILES):
+                if vector_relu(k, n):
+                    nc.vector.tensor_scalar(
+                        out=out_rows[k][:, n, :],
+                        in0=out_banks[k, n][:],
+                        scalar1=0.0,
+                        scalar2=None,
+                        op0=MAX,
+                    )
+
+        def store(k):
+            result = out_rows[k]
+            rows = out_view[k // UNITS_PER_LOAD, k % UNITS_PER_LOAD]
+            if k == UNITS - 1:
+                for n in range(UNIT_TILES):
+                    nc.sync.dma_start(out=rows[:, n, :], in_=result[:, n, :])
+            else:
+                nc.sync.dma_start(out=rows, in_=result[:])
+
+        def run_after(last, stage, k):
+            if k > last:
+                run(stage, k)
 
         def run(stage, k):
             if 0 <= k < UNITS:
                 stage(k)
 
-        for step in range(UNITS + PROJECT_LAG):
-            run(sum_rows, step)
-            run(pool_features, step - POOL_LAG)
-            run(gather_words, step - GATHER_LAG)
-            run(regroup_pooled, step - POOL_LAG)
+        fold_rows(0)
+        sum_rows(0)
+        group_x(nc.vector.tensor_copy, 0, 192)
+        group_x(nc.scalar.copy, 384, K)
+        invert_sums(0)
+        group_x(nc.vector.tensor_copy, 192, 384)
+        scale_rows(0)
+        fold_rows(1)
+        transpose_rows(0)
+        sum_rows(1)
+        gather_words(0)
+        invert_sums(1)
+        quantise_x()
+        scale_rows(1)
+        fold_rows(2)
+        transpose_rows(1)
+        sum_rows(2)
+        quantise_adj(0)
+        gather_words(1)
+        invert_sums(2)
+        pool_features(0)
+        regroup_pooled(0)
+        quantise_adj(1)
+        fold_rows(3)
+        scale_rows(2)
+        group_w()
+        sum_rows(3)
+        fold_rows(4)
+        for step in range(3, UNITS + PROJECT_LAG):
+            run_after(4, fold_rows, step + 2)
             run(invert_sums, step)
             run(project, step - PROJECT_LAG)
+            run(relu_scalar, step - PROJECT_LAG)
+            run_after(0, pool_features, step - POOL_LAG)
+            run_after(0, regroup_pooled, step - POOL_LAG)
+            run_after(1, transpose_rows, step - 1)
+            run(sum_rows, step + 1)
+            run_after(1, gather_words, step - GATHER_LAG)
+            run(relu_vector, step - PROJECT_LAG)
+            run(store, step - PROJECT_LAG)
             run(quantise_pooled, step - REQUANT_LAG)
-            run(relu_and_store, step - PROJECT_LAG)
             run(scale_rows, step)
-            run(transpose_rows, step)
-            run(quantise_adj, step - GATHER_LAG)
+            run_after(1, quantise_adj, step - GATHER_LAG)
             if step == W_STEP:
                 quantise_w()

@@ -26,7 +26,7 @@ UNIT_COLS = UNIT_TILES * P
 UNITS = GATHERERS // UNIT_COLS
 LOADS = GATHERERS // (LOAD_TILES * P)
 UNITS_PER_LOAD = LOAD_TILES // UNIT_TILES
-SUM_COLS = 64
+SUM_COLS = 128
 
 GATHER_LAG = 2
 POOL_LAG = 3

@@ -41,11 +41,11 @@ def tensor_sums(k, n):
 
 
 def vector_relu(k, n):
-    return (k % 4 == 3 and n == 1) or (k >= UNITS - 4 and n == 1)
+    return (k % 4 == 3 or k >= UNITS - 5) and n == 1
 
 
 def vector_regroup(k, n):
-    return k == UNITS - 1 and n == 1
+    return k >= UNITS - 2 and n == 1
 
 
 def tile_egcn_pa_t_kernel(tc, x, adjacency, W, out):
@@ -55,10 +55,7 @@ def tile_egcn_pa_t_kernel(tc, x, adjacency, W, out):
         adj = ctx.enter_context(tc.tile_pool(name="adj", bufs=LOADS))
         work = ctx.enter_context(tc.tile_pool(name="work", bufs=6))
         results = ctx.enter_context(tc.tile_pool(name="results", bufs=8))
-        psum_t = ctx.enter_context(tc.psum_pool(name="psum_t", bufs=2))
-        psum_pool = ctx.enter_context(tc.psum_pool(name="psum_pool", bufs=2))
-        psum_out = ctx.enter_context(tc.psum_pool(name="psum_out", bufs=2))
-        psum_sum = ctx.enter_context(tc.psum_pool(name="psum_sum", bufs=2))
+        psum = ctx.enter_context(tc.psum_pool(name="psum", bufs=8))
         ctx.enter_context(tc.manual_schedule())
 
         adj_view = adjacency.rearrange("(s p n) j -> s p n j", p=P, n=LOAD_TILES)
@@ -126,12 +123,15 @@ def tile_egcn_pa_t_kernel(tc, x, adjacency, W, out):
         pooled_banks, pooled_grouped, pooled_codes, pooled_scales = {}, {}, {}, {}
         out_banks, out_rows = {}, {}
 
+        def new_bank():
+            bank = psum.tile([P, K], F32, name="bank")
+            return bank
+
         def unit_rows(k, n):
             return adj_rows[k // UNITS_PER_LOAD][:, (k % UNITS_PER_LOAD) * UNIT_TILES + n, :]
 
         def fold_rows(k):
-            whole_bank = psum_sum.tile([P, K], F32)
-            bank = whole_bank[:, : UNIT_TILES * SUM_COLS].rearrange(
+            bank = new_bank()[:, : UNIT_TILES * SUM_COLS].rearrange(
                 "p (n w) -> p n w", n=UNIT_TILES
             )
             blocks = K // SUM_COLS
@@ -188,7 +188,7 @@ def tile_egcn_pa_t_kernel(tc, x, adjacency, W, out):
 
         def transpose_rows(k):
             words = norm_rows[k][:].bitcast(F32)
-            bank = psum_t.tile([P, UNIT_TILES, 2, P], F32)
+            bank = new_bank()[:].rearrange("p (n u i) -> p n u i", n=UNIT_TILES, u=2)
             for n in range(UNIT_TILES):
                 for u in range(2):
                     nc.tensor.transpose(
@@ -203,7 +203,7 @@ def tile_egcn_pa_t_kernel(tc, x, adjacency, W, out):
             copy = nc.scalar.copy if k < SCALAR_GATHERS else nc.vector.tensor_copy
             copy(
                 out=grouped[:].bitcast(F32).rearrange("p (n i) u -> p n i u", n=UNIT_TILES),
-                in_=turned[k][:].rearrange("p n u i -> p n i u"),
+                in_=turned[k].rearrange("p n u i -> p n i u"),
             )
             adj_grouped[k] = grouped
 
@@ -220,7 +220,7 @@ def tile_egcn_pa_t_kernel(tc, x, adjacency, W, out):
         def pool_features(k):
             for n in range(UNIT_TILES):
                 cols = slice(n * P, (n + 1) * P)
-                bank = psum_pool.tile([P, PACK, P], F32)
+                bank = new_bank()[:].rearrange("p (t i) -> p t i", t=PACK)
                 for t in range(PACK):
                     feats = slice(t * P, (t + 1) * P)
                     nc.tensor.matmul_mx(
@@ -238,7 +238,7 @@ def tile_egcn_pa_t_kernel(tc, x, adjacency, W, out):
             grouped2 = work.tile([P, UNIT_COLS, PACK], BF16, align_bytes=64)
             for n in range(UNIT_TILES):
                 dst = grouped2[:, n * P : (n + 1) * P, :]
-                src = pooled_banks[k, n][:].rearrange("p t i -> p i t")
+                src = pooled_banks[k, n].rearrange("p t i -> p i t")
                 if vector_regroup(k, n):
                     nc.vector.tensor_copy(out=dst, in_=src)
                 else:
@@ -258,7 +258,7 @@ def tile_egcn_pa_t_kernel(tc, x, adjacency, W, out):
         def project(k):
             for n in range(UNIT_TILES):
                 cols = slice(n * P, (n + 1) * P)
-                acc = psum_out.tile([P, K], F32)
+                acc = new_bank()
                 nc.tensor.matmul_mx(
                     out=acc[:],
                     lhsT=pooled_codes[k][:, cols].bitcast(FP8X4),
@@ -333,8 +333,7 @@ def tile_egcn_pa_t_kernel(tc, x, adjacency, W, out):
         group_w()
         sum_rows(3)
         fold_rows(4)
-        for step in range(3, UNITS + PROJECT_LAG):
-            run_after(4, fold_rows, step + 2)
+        for step in range(3, UNITS):
             run(invert_sums, step)
             run(project, step - PROJECT_LAG)
             run(relu_scalar, step - PROJECT_LAG)
@@ -342,6 +341,7 @@ def tile_egcn_pa_t_kernel(tc, x, adjacency, W, out):
             run_after(0, regroup_pooled, step - POOL_LAG)
             run_after(1, transpose_rows, step - 1)
             run(sum_rows, step + 1)
+            run_after(4, fold_rows, step + 2)
             run_after(1, gather_words, step - GATHER_LAG)
             run(relu_vector, step - PROJECT_LAG)
             run(store, step - PROJECT_LAG)
@@ -350,3 +350,40 @@ def tile_egcn_pa_t_kernel(tc, x, adjacency, W, out):
             run_after(1, quantise_adj, step - GATHER_LAG)
             if step == W_STEP:
                 quantise_w()
+
+        last = UNITS - 1
+        project(last - 4)
+        relu_scalar(last - 4)
+        pool_features(last - 2)
+        transpose_rows(last)
+        gather_words(last - 1)
+        relu_vector(last - 4)
+        store(last - 4)
+        quantise_pooled(last - 3)
+        quantise_adj(last - 1)
+        gather_words(last)
+        regroup_pooled(last - 2)
+        project(last - 3)
+        relu_scalar(last - 3)
+        quantise_adj(last)
+        pool_features(last - 1)
+        quantise_pooled(last - 2)
+        relu_vector(last - 3)
+        store(last - 3)
+        regroup_pooled(last - 1)
+        pool_features(last)
+        project(last - 2)
+        regroup_pooled(last)
+        quantise_pooled(last - 1)
+        relu_scalar(last - 2)
+        relu_vector(last - 2)
+        store(last - 2)
+        project(last - 1)
+        quantise_pooled(last)
+        relu_scalar(last - 1)
+        relu_vector(last - 1)
+        store(last - 1)
+        project(last)
+        relu_scalar(last)
+        relu_vector(last)
+        store(last)

@@ -44,6 +44,10 @@ def vector_relu(k, n):
     return (k % 4 == 3 or k >= UNITS - 5) and n == 1
 
 
+def gpsimd_scale(k, n):
+    return k >= 3 and n == 0
+
+
 def vector_regroup(k, n):
     return k >= UNITS - 2 and n == 1
 
@@ -178,13 +182,26 @@ def tile_egcn_pa_t_kernel(tc, x, adjacency, W, out):
 
         def scale_rows(k):
             for n in range(UNIT_TILES):
-                nc.vector.tensor_scalar(
-                    out=norm_rows[k][:, n, :],
-                    in0=unit_rows(k, n),
-                    scalar1=inverses[k][:, n : n + 1],
-                    scalar2=None,
-                    op0=MULT,
-                )
+                if not gpsimd_scale(k, n):
+                    nc.vector.tensor_scalar(
+                        out=norm_rows[k][:, n, :],
+                        in0=unit_rows(k, n),
+                        scalar1=inverses[k][:, n : n + 1],
+                        scalar2=None,
+                        op0=MULT,
+                    )
+
+        def scale_rows_gpsimd(k):
+            for n in range(UNIT_TILES):
+                if gpsimd_scale(k, n):
+                    nc.gpsimd.tensor_scalar(
+                        out=norm_rows[k][:, n, :],
+                        in0=unit_rows(k, n),
+                        scalar1=inverses[k][:, n : n + 1],
+                        scalar2=0.0,
+                        op0=MULT,
+                        op1=ADD,
+                    )
 
         def transpose_rows(k):
             words = norm_rows[k][:].bitcast(F32)
@@ -335,6 +352,7 @@ def tile_egcn_pa_t_kernel(tc, x, adjacency, W, out):
         fold_rows(4)
         for step in range(3, UNITS):
             run(invert_sums, step)
+            run(scale_rows_gpsimd, step)
             run(project, step - PROJECT_LAG)
             run(relu_scalar, step - PROJECT_LAG)
             run_after(0, pool_features, step - POOL_LAG)

@@ -33,15 +33,15 @@ POOL_LAG = 3
 REQUANT_LAG = 4
 PROJECT_LAG = 5
 SCALAR_GATHERS = 2
-W_STEP = 4
+W_STEP = 3
 
 
 def tensor_sums(k, n):
-    return n == 1 or 0 < k < 3
+    return (n == 1 and k % 4 != 0) or 0 < k < 3
 
 
 def vector_relu(k, n):
-    return (k % 4 == 3 or k >= UNITS - 5) and n == 1
+    return (k % 4 == 3 or k >= UNITS - 6) and n == 1
 
 
 def gpsimd_scale(k, n):
@@ -79,16 +79,17 @@ def tile_egcn_pa_t_kernel(tc, x, adjacency, W, out):
                     in_=x.rearrange("(u p e) f -> p u (e f)", u=2, p=P, e=2),
                 )
                 nc.sync.dma_start(out=a_rows[:, UNIT_TILES:, :], in_=adj_view[s, :, UNIT_TILES:, :])
-            else:
-                nc.sync.dma_start(out=a_rows[:], in_=adj_view[s])
-            adj_rows.append(a_rows)
-            if s == 1:
                 nc.sync.dma_start(
                     out=w_raw[:], in_=W.rearrange("(t p) g -> p t g", t=PACK, p=P)
                 )
+            else:
+                nc.sync.dma_start(out=a_rows[:], in_=adj_view[s])
+            adj_rows.append(a_rows)
 
         ident_bf16 = keep.tile([P, P], BF16)
         make_identity(nc, ident_bf16[:])
+        filler = keep.tile([P, K], BF16)
+        nc.vector.memset(filler[:], 0.0)
         identity = keep.tile([P, P], F32)
         make_identity(nc, identity[:])
 
@@ -112,8 +113,11 @@ def tile_egcn_pa_t_kernel(tc, x, adjacency, W, out):
                 in_=x_grouped[:].rearrange("p f t -> p (f t)"),
             )
 
-        def group_w():
-            nc.scalar.copy(out=w_grouped[:], in_=w_raw[:].rearrange("p t g -> p g t"))
+        def group_w(quarter):
+            cols = slice(quarter * P, (quarter + 1) * P)
+            nc.scalar.copy(
+                out=w_grouped[:, cols, :], in_=w_raw[:, :, cols].rearrange("p t g -> p g t")
+            )
 
         def quantise_w():
             nc.vector.quantize_mx(
@@ -133,6 +137,13 @@ def tile_egcn_pa_t_kernel(tc, x, adjacency, W, out):
 
         def unit_rows(k, n):
             return adj_rows[k // UNITS_PER_LOAD][:, (k % UNITS_PER_LOAD) * UNIT_TILES + n, :]
+
+        def keep_busy(count):
+            bank = new_bank()
+            for repeat in range(count):
+                nc.tensor.matmul(
+                    out=bank[:], lhsT=filler[:, :P], rhs=filler[:], start=True, stop=True
+                )
 
         def fold_rows(k):
             bank = new_bank()[:, : UNIT_TILES * SUM_COLS].rearrange(
@@ -308,7 +319,7 @@ def tile_egcn_pa_t_kernel(tc, x, adjacency, W, out):
         def store(k):
             result = out_rows[k]
             rows = out_view[k // UNITS_PER_LOAD, k % UNITS_PER_LOAD]
-            if k == UNITS - 1:
+            if k >= UNITS - 3:
                 for n in range(UNIT_TILES):
                     nc.sync.dma_start(out=rows[:, n, :], in_=result[:, n, :])
             else:
@@ -322,7 +333,9 @@ def tile_egcn_pa_t_kernel(tc, x, adjacency, W, out):
             if 0 <= k < UNITS:
                 stage(k)
 
+        keep_busy(4)
         fold_rows(0)
+        keep_busy(2)
         sum_rows(0)
         group_x(nc.vector.tensor_copy, 0, 192)
         group_x(nc.scalar.copy, 384, K)
@@ -331,23 +344,28 @@ def tile_egcn_pa_t_kernel(tc, x, adjacency, W, out):
         scale_rows(0)
         fold_rows(1)
         transpose_rows(0)
+        group_w(0)
+        keep_busy(1)
         sum_rows(1)
         gather_words(0)
+        group_w(1)
         invert_sums(1)
         quantise_x()
         scale_rows(1)
         fold_rows(2)
         transpose_rows(1)
+        keep_busy(1)
         sum_rows(2)
         quantise_adj(0)
         gather_words(1)
+        group_w(2)
         invert_sums(2)
         pool_features(0)
         regroup_pooled(0)
         quantise_adj(1)
         fold_rows(3)
         scale_rows(2)
-        group_w()
+        group_w(3)
         sum_rows(3)
         fold_rows(4)
         for step in range(3, UNITS):

@@ -33,23 +33,23 @@ POOL_LAG = 3
 REQUANT_LAG = 4
 PROJECT_LAG = 5
 SCALAR_GATHERS = 2
-W_STEP = 3
+W_STEP = 4
 
 
 def tensor_sums(k, n):
-    return (n == 1 and k % 4 != 0) or 0 < k < 3
+    return (n == 1 and k > 3) or 0 < k < 3
 
 
 def vector_relu(k, n):
-    return (k % 4 == 3 or k >= UNITS - 6) and n == 1
+    return (k % 3 == 2 or k >= UNITS - 6) and n == 1
 
 
 def gpsimd_scale(k, n):
-    return k >= 3 and n == 0
+    return k >= 4 and n == 0
 
 
 def vector_regroup(k, n):
-    return k >= UNITS - 2 and n == 1
+    return k >= UNITS - 1 and n == 1
 
 
 def tile_egcn_pa_t_kernel(tc, x, adjacency, W, out):
@@ -334,9 +334,8 @@ def tile_egcn_pa_t_kernel(tc, x, adjacency, W, out):
                 stage(k)
 
         keep_busy(4)
-        fold_rows(0)
-        keep_busy(2)
         sum_rows(0)
+        keep_busy(2)
         group_x(nc.vector.tensor_copy, 0, 192)
         group_x(nc.scalar.copy, 384, K)
         invert_sums(0)
@@ -344,8 +343,8 @@ def tile_egcn_pa_t_kernel(tc, x, adjacency, W, out):
         scale_rows(0)
         fold_rows(1)
         transpose_rows(0)
-        group_w(0)
         keep_busy(1)
+        group_w(0)
         sum_rows(1)
         gather_words(0)
         group_w(1)
@@ -355,18 +354,17 @@ def tile_egcn_pa_t_kernel(tc, x, adjacency, W, out):
         fold_rows(2)
         transpose_rows(1)
         keep_busy(1)
-        sum_rows(2)
         quantise_adj(0)
+        sum_rows(2)
         gather_words(1)
         group_w(2)
+        sum_rows(3)
         invert_sums(2)
         pool_features(0)
         regroup_pooled(0)
         quantise_adj(1)
-        fold_rows(3)
         scale_rows(2)
         group_w(3)
-        sum_rows(3)
         fold_rows(4)
         for step in range(3, UNITS):
             run(invert_sums, step)
@@ -375,17 +373,17 @@ def tile_egcn_pa_t_kernel(tc, x, adjacency, W, out):
             run(relu_scalar, step - PROJECT_LAG)
             run_after(0, pool_features, step - POOL_LAG)
             run_after(0, regroup_pooled, step - POOL_LAG)
-            run_after(1, transpose_rows, step - 1)
             run(sum_rows, step + 1)
             run_after(4, fold_rows, step + 2)
+            if step == W_STEP:
+                quantise_w()
+            run_after(1, transpose_rows, step - 1)
             run_after(1, gather_words, step - GATHER_LAG)
             run(relu_vector, step - PROJECT_LAG)
             run(store, step - PROJECT_LAG)
             run(quantise_pooled, step - REQUANT_LAG)
             run(scale_rows, step)
             run_after(1, quantise_adj, step - GATHER_LAG)
-            if step == W_STEP:
-                quantise_w()
 
         last = UNITS - 1
         project(last - 4)
@@ -409,8 +407,8 @@ def tile_egcn_pa_t_kernel(tc, x, adjacency, W, out):
         regroup_pooled(last - 1)
         pool_features(last)
         project(last - 2)
-        regroup_pooled(last)
         quantise_pooled(last - 1)
+        regroup_pooled(last)
         relu_scalar(last - 2)
         relu_vector(last - 2)
         store(last - 2)

@@ -12,6 +12,7 @@ MULT = mybir.AluOpType.mult
 ADD = mybir.AluOpType.add
 MAX = mybir.AluOpType.max
 AXIS_X = mybir.AxisListType.X
+COPY = mybir.ActivationFunctionType.Copy
 RELU = mybir.ActivationFunctionType.Relu
 
 P = 128
@@ -32,12 +33,12 @@ GATHER_LAG = 2
 POOL_LAG = 3
 REQUANT_LAG = 4
 PROJECT_LAG = 5
-SCALAR_GATHERS = 2
+SCALAR_GATHERS = (0, 1, 2, 3)
 W_STEP = 4
 
 
 def tensor_sums(k, n):
-    return (n == 1 and k > 3) or 0 < k < 3
+    return n == 1 and k > 1
 
 
 def vector_relu(k, n):
@@ -45,7 +46,7 @@ def vector_relu(k, n):
 
 
 def gpsimd_scale(k, n):
-    return k >= 4 and n == 0
+    return k >= 6 and n == 0
 
 
 def vector_regroup(k, n):
@@ -73,23 +74,23 @@ def tile_egcn_pa_t_kernel(tc, x, adjacency, W, out):
         for s in range(LOADS):
             a_rows = adj.tile([P, LOAD_TILES, K], BF16)
             if s == 0:
-                nc.sync.dma_start(out=a_rows[:, :UNIT_TILES, :], in_=adj_view[s, :, :UNIT_TILES, :])
+                for h in range(UNITS_PER_LOAD):
+                    tiles = slice(h * UNIT_TILES, (h + 1) * UNIT_TILES)
+                    nc.sync.dma_start(out=a_rows[:, tiles, :], in_=adj_view[s, :, tiles, :])
                 nc.sync.dma_start(
                     out=x_raw[:].rearrange("p (u e) f -> p u (e f)", u=2, e=2),
                     in_=x.rearrange("(u p e) f -> p u (e f)", u=2, p=P, e=2),
                 )
-                nc.sync.dma_start(out=a_rows[:, UNIT_TILES:, :], in_=adj_view[s, :, UNIT_TILES:, :])
+            else:
+                nc.sync.dma_start(out=a_rows[:], in_=adj_view[s])
+            if s == 1:
                 nc.sync.dma_start(
                     out=w_raw[:], in_=W.rearrange("(t p) g -> p t g", t=PACK, p=P)
                 )
-            else:
-                nc.sync.dma_start(out=a_rows[:], in_=adj_view[s])
             adj_rows.append(a_rows)
 
         ident_bf16 = keep.tile([P, P], BF16)
         make_identity(nc, ident_bf16[:])
-        filler = keep.tile([P, K], BF16)
-        nc.vector.memset(filler[:], 0.0)
         identity = keep.tile([P, P], F32)
         make_identity(nc, identity[:])
 
@@ -113,9 +114,9 @@ def tile_egcn_pa_t_kernel(tc, x, adjacency, W, out):
                 in_=x_grouped[:].rearrange("p f t -> p (f t)"),
             )
 
-        def group_w(quarter):
+        def group_w(engine_copy, quarter):
             cols = slice(quarter * P, (quarter + 1) * P)
-            nc.scalar.copy(
+            engine_copy(
                 out=w_grouped[:, cols, :], in_=w_raw[:, :, cols].rearrange("p t g -> p g t")
             )
 
@@ -138,11 +139,11 @@ def tile_egcn_pa_t_kernel(tc, x, adjacency, W, out):
         def unit_rows(k, n):
             return adj_rows[k // UNITS_PER_LOAD][:, (k % UNITS_PER_LOAD) * UNIT_TILES + n, :]
 
-        def keep_busy(count):
+        def keep_busy(count, k, n):
             bank = new_bank()
             for repeat in range(count):
                 nc.tensor.matmul(
-                    out=bank[:], lhsT=filler[:, :P], rhs=filler[:], start=True, stop=True
+                    out=bank[:], lhsT=ident_bf16[:], rhs=unit_rows(k, n), start=True, stop=True
                 )
 
         def fold_rows(k):
@@ -163,13 +164,15 @@ def tile_egcn_pa_t_kernel(tc, x, adjacency, W, out):
                     )
             folded[k] = bank
 
-        def sum_rows(k):
+        def sum_rows(k, skip=None):
             rows = work.tile([P, UNIT_TILES, K], BF16)
             deg = work.tile([P, UNIT_TILES], F32)
             if all(tensor_sums(k, n) for n in range(UNIT_TILES)):
                 nc.vector.tensor_reduce(out=deg[:], in_=folded[k], axis=AXIS_X, op=ADD)
             else:
                 for n in range(UNIT_TILES):
+                    if n == skip:
+                        continue
                     if tensor_sums(k, n):
                         nc.vector.tensor_reduce(
                             out=deg[:, n : n + 1], in_=folded[k][:, n, :], axis=AXIS_X, op=ADD
@@ -185,6 +188,19 @@ def tile_egcn_pa_t_kernel(tc, x, adjacency, W, out):
                         accum_out=deg[:, n : n + 1],
                     )
             norm_rows[k], degrees[k] = rows, deg
+
+        def sum_folded(k):
+            nc.vector.tensor_reduce(
+                out=degrees[k][:, 1:2], in_=folded[k][:, 1, :], axis=AXIS_X, op=ADD
+            )
+
+        def scalar_sum(k, n):
+            nc.scalar.activation(
+                out=norm_rows[k][:, n, :],
+                in_=unit_rows(k, n),
+                func=COPY,
+                accum_out=degrees[k][:, n : n + 1],
+            )
 
         def invert_sums(k):
             inv = work.tile([P, UNIT_TILES], F32)
@@ -228,7 +244,7 @@ def tile_egcn_pa_t_kernel(tc, x, adjacency, W, out):
 
         def gather_words(k):
             grouped = work.tile([P, UNIT_COLS, PACK], BF16, align_bytes=64)
-            copy = nc.scalar.copy if k < SCALAR_GATHERS else nc.vector.tensor_copy
+            copy = nc.scalar.copy if k in SCALAR_GATHERS else nc.vector.tensor_copy
             copy(
                 out=grouped[:].bitcast(F32).rearrange("p (n i) u -> p n i u", n=UNIT_TILES),
                 in_=turned[k].rearrange("p n u i -> p n i u"),
@@ -325,99 +341,116 @@ def tile_egcn_pa_t_kernel(tc, x, adjacency, W, out):
             else:
                 nc.sync.dma_start(out=rows, in_=result[:])
 
-        def run_after(last, stage, k):
-            if k > last:
-                run(stage, k)
+        done = set()
 
         def run(stage, k):
-            if 0 <= k < UNITS:
+            if 0 <= k < UNITS and (stage, k) not in done:
+                done.add((stage, k))
                 stage(k)
 
-        keep_busy(4)
-        sum_rows(0)
-        keep_busy(2)
-        group_x(nc.vector.tensor_copy, 0, 192)
-        group_x(nc.scalar.copy, 384, K)
-        invert_sums(0)
-        group_x(nc.vector.tensor_copy, 192, 384)
-        scale_rows(0)
-        fold_rows(1)
-        transpose_rows(0)
-        keep_busy(1)
-        group_w(0)
-        sum_rows(1)
-        gather_words(0)
-        group_w(1)
-        invert_sums(1)
+        keep_busy(4, 0, 0)
+        sum_rows(0, skip=1)
+        done.add((sum_rows, 0))
+        scalar_sum(0, 1)
+        run(sum_rows, 1)
+        run(invert_sums, 0)
+        run(scale_rows, 0)
+        run(invert_sums, 1)
+        run(transpose_rows, 0)
+        group_x(nc.scalar.copy, 256, K)
+        group_x(nc.vector.tensor_copy, 0, 128)
+        run(scale_rows, 1)
+        run(transpose_rows, 1)
+        group_x(nc.vector.tensor_copy, 128, 256)
+        run(gather_words, 0)
+        run(gather_words, 1)
         quantise_x()
-        scale_rows(1)
-        fold_rows(2)
-        transpose_rows(1)
-        keep_busy(1)
-        quantise_adj(0)
-        sum_rows(2)
-        gather_words(1)
-        group_w(2)
-        sum_rows(3)
-        invert_sums(2)
-        pool_features(0)
-        regroup_pooled(0)
-        quantise_adj(1)
-        scale_rows(2)
-        group_w(3)
-        fold_rows(4)
-        for step in range(3, UNITS):
+        run(fold_rows, 2)
+        run(fold_rows, 3)
+        run(quantise_adj, 0)
+        run(sum_rows, 2)
+        run(quantise_adj, 1)
+        run(pool_features, 0)
+        group_w(nc.scalar.copy, 0)
+        group_w(nc.scalar.copy, 1)
+        run(regroup_pooled, 0)
+        run(pool_features, 1)
+        run(regroup_pooled, 1)
+        run(sum_rows, 3)
+        run(invert_sums, 2)
+        run(invert_sums, 3)
+        run(scale_rows, 2)
+        run(scale_rows, 3)
+        run(transpose_rows, 2)
+        run(transpose_rows, 3)
+        run(fold_rows, 4)
+        group_w(nc.vector.tensor_copy, 2)
+        group_w(nc.vector.tensor_copy, 3)
+        run(fold_rows, 5)
+        sum_rows(4, skip=1)
+        done.add((sum_rows, 4))
+        run(gather_words, 2)
+        run(gather_words, 3)
+        quantise_w()
+        run(quantise_pooled, 0)
+        run(quantise_adj, 2)
+        sum_folded(4)
+        run(quantise_pooled, 1)
+        run(quantise_adj, 3)
+        run(invert_sums, 4)
+        run(project, 0)
+        run(pool_features, 2)
+        run(relu_scalar, 0)
+        for step in range(4, UNITS):
             run(invert_sums, step)
             run(scale_rows_gpsimd, step)
             run(project, step - PROJECT_LAG)
             run(relu_scalar, step - PROJECT_LAG)
-            run_after(0, pool_features, step - POOL_LAG)
-            run_after(0, regroup_pooled, step - POOL_LAG)
+            run(pool_features, step - POOL_LAG)
+            run(regroup_pooled, step - POOL_LAG)
             run(sum_rows, step + 1)
-            run_after(4, fold_rows, step + 2)
-            if step == W_STEP:
-                quantise_w()
-            run_after(1, transpose_rows, step - 1)
-            run_after(1, gather_words, step - GATHER_LAG)
+            run(fold_rows, step + 2)
+            run(transpose_rows, step - 1)
+            run(gather_words, step - GATHER_LAG)
             run(relu_vector, step - PROJECT_LAG)
             run(store, step - PROJECT_LAG)
             run(quantise_pooled, step - REQUANT_LAG)
             run(scale_rows, step)
-            run_after(1, quantise_adj, step - GATHER_LAG)
+            run(quantise_adj, step - GATHER_LAG)
 
         last = UNITS - 1
-        project(last - 4)
-        relu_scalar(last - 4)
-        pool_features(last - 2)
-        transpose_rows(last)
-        gather_words(last - 1)
-        relu_vector(last - 4)
-        store(last - 4)
-        quantise_pooled(last - 3)
-        quantise_adj(last - 1)
-        gather_words(last)
-        regroup_pooled(last - 2)
-        project(last - 3)
-        relu_scalar(last - 3)
-        quantise_adj(last)
-        pool_features(last - 1)
-        quantise_pooled(last - 2)
-        relu_vector(last - 3)
-        store(last - 3)
-        regroup_pooled(last - 1)
-        pool_features(last)
-        project(last - 2)
-        quantise_pooled(last - 1)
-        regroup_pooled(last)
-        relu_scalar(last - 2)
-        relu_vector(last - 2)
-        store(last - 2)
-        project(last - 1)
-        quantise_pooled(last)
-        relu_scalar(last - 1)
-        relu_vector(last - 1)
-        store(last - 1)
-        project(last)
-        relu_scalar(last)
-        relu_vector(last)
-        store(last)
+        run(project, last - 4)
+        run(relu_scalar, last - 4)
+        run(pool_features, last - 2)
+        run(transpose_rows, last)
+        run(gather_words, last - 1)
+        run(relu_vector, last - 4)
+        run(store, last - 4)
+        run(quantise_pooled, last - 3)
+        run(quantise_adj, last - 1)
+        run(gather_words, last)
+        run(regroup_pooled, last - 2)
+        run(project, last - 3)
+        run(relu_scalar, last - 3)
+        run(quantise_adj, last)
+        run(pool_features, last - 1)
+        run(quantise_pooled, last - 2)
+        run(relu_vector, last - 3)
+        run(store, last - 3)
+        run(regroup_pooled, last - 1)
+        run(pool_features, last)
+        run(project, last - 2)
+        run(quantise_pooled, last - 1)
+        run(regroup_pooled, last)
+        run(relu_scalar, last - 2)
+        run(relu_vector, last - 2)
+        run(store, last - 2)
+        run(project, last - 1)
+        run(quantise_pooled, last)
+        run(relu_scalar, last - 1)
+        run(relu_vector, last - 1)
+        run(store, last - 1)
+        run(project, last)
+        run(relu_scalar, last)
+        run(relu_vector, last)
+        run(store, last)

@@ -103,8 +103,8 @@ def tile_egcn_pa_t_kernel(tc, x, adjacency, W, out):
 
         def group_x(engine_copy, first, last):
             engine_copy(
-                out=x_grouped[:, first:last, :],
-                in_=x_raw[:, :, first:last].rearrange("p t f -> p f t"),
+                out=x_grouped[:, first:last, :].rearrange("p (f i) t -> p f t i", i=PACK),
+                in_=x_raw[:, :, first:last].rearrange("p t (f i) -> p f t i", i=PACK),
             )
 
         def quantise_x():
@@ -117,7 +117,8 @@ def tile_egcn_pa_t_kernel(tc, x, adjacency, W, out):
         def group_w(engine_copy, quarter):
             cols = slice(quarter * P, (quarter + 1) * P)
             engine_copy(
-                out=w_grouped[:, cols, :], in_=w_raw[:, :, cols].rearrange("p t g -> p g t")
+                out=w_grouped[:, cols, :].rearrange("p (g i) t -> p g t i", i=PACK),
+                in_=w_raw[:, :, cols].rearrange("p t (g i) -> p g t i", i=PACK),
             )
 
         def quantise_w():

@@ -38,7 +38,7 @@ W_STEP = 4
 
 
 def tensor_sums(k, n):
-    return n == 1 and k > 1
+    return n == 1 and k > 1 or k == 5
 
 
 def vector_relu(k, n):
@@ -112,6 +112,11 @@ def tile_egcn_pa_t_kernel(tc, x, adjacency, W, out):
                 out=x_codes[:].bitcast(FP8X4),
                 scales=x_scales[:],
                 in_=x_grouped[:].rearrange("p f t -> p (f t)"),
+            )
+
+        def gpsimd_copy(out, in_):
+            nc.gpsimd.tensor_scalar(
+                out=out, in0=in_, scalar1=1.0, scalar2=0.0, op0=MULT, op1=ADD
             )
 
         def group_w(engine_copy, quarter):
@@ -372,28 +377,28 @@ def tile_egcn_pa_t_kernel(tc, x, adjacency, W, out):
         run(sum_rows, 2)
         run(quantise_adj, 1)
         run(pool_features, 0)
-        group_w(nc.scalar.copy, 0)
+        group_w(gpsimd_copy, 0)
         group_w(nc.scalar.copy, 1)
         run(regroup_pooled, 0)
         run(pool_features, 1)
         run(regroup_pooled, 1)
         run(sum_rows, 3)
         run(invert_sums, 2)
+        group_w(nc.vector.tensor_copy, 2)
         run(invert_sums, 3)
+        group_w(nc.vector.tensor_copy, 3)
         run(scale_rows, 2)
         run(scale_rows, 3)
         run(transpose_rows, 2)
         run(transpose_rows, 3)
         run(fold_rows, 4)
-        group_w(nc.vector.tensor_copy, 2)
-        group_w(nc.vector.tensor_copy, 3)
         run(fold_rows, 5)
+        quantise_w()
+        run(quantise_pooled, 0)
         sum_rows(4, skip=1)
         done.add((sum_rows, 4))
         run(gather_words, 2)
         run(gather_words, 3)
-        quantise_w()
-        run(quantise_pooled, 0)
         run(quantise_adj, 2)
         sum_folded(4)
         run(quantise_pooled, 1)

@@ -422,6 +422,8 @@ def tile_egcn_pa_t_kernel(tc, x, adjacency, W, out):
             run(store, step - PROJECT_LAG)
             run(quantise_pooled, step - REQUANT_LAG)
             run(scale_rows, step)
+            run(invert_sums, step + 1)
+            run(scale_rows_gpsimd, step + 1)
             run(quantise_adj, step - GATHER_LAG)
 
         last = UNITS - 1

@@ -46,7 +46,7 @@ def vector_relu(k, n):
 
 
 def gpsimd_scale(k, n):
-    return k >= 6 and n == 0
+    return k >= 6 and (n == 0 or k % 3 == 1)
 
 
 def vector_regroup(k, n):

from contextlib import ExitStack

import concourse.mybir as mybir
from concourse.masks import make_identity

BF16 = mybir.dt.bfloat16
F32 = mybir.dt.float32
U32 = mybir.dt.uint32
U8 = mybir.dt.uint8
FP8X4 = mybir.dt.float8_e4m3fn_x4
MULT = mybir.AluOpType.mult
ADD = mybir.AluOpType.add
MAX = mybir.AluOpType.max
AXIS_X = mybir.AxisListType.X
COPY = mybir.ActivationFunctionType.Copy
RELU = mybir.ActivationFunctionType.Relu

P = 128
PACK = 4
GATHERERS = 8192
K = P * PACK
FLOPS = 2 * GATHERERS * K * K * 2

LOAD_TILES = 4
UNIT_TILES = 2
UNIT_COLS = UNIT_TILES * P
UNITS = GATHERERS // UNIT_COLS
LOADS = GATHERERS // (LOAD_TILES * P)
UNITS_PER_LOAD = LOAD_TILES // UNIT_TILES
SUM_COLS = 128

GATHER_LAG = 2
POOL_LAG = 3
REQUANT_LAG = 4
PROJECT_LAG = 5
SCALAR_GATHERS = (0, 1, 2, 3)
W_STEP = 4


def tensor_sums(k, n):
    return n == 1 and k > 1 or k == 5


def vector_relu(k, n):
    return (k % 3 == 2 or k >= UNITS - 6) and n == 1


def gpsimd_scale(k, n):
    return k >= 6 and (n == 0 or k % 3 == 1)


def vector_regroup(k, n):
    return k >= UNITS - 1 and n == 1


def tile_egcn_pa_t_kernel(tc, x, adjacency, W, out):
    nc = tc.nc
    with ExitStack() as ctx:
        keep = ctx.enter_context(tc.tile_pool(name="keep", bufs=1))
        adj = ctx.enter_context(tc.tile_pool(name="adj", bufs=LOADS))
        work = ctx.enter_context(tc.tile_pool(name="work", bufs=6))
        results = ctx.enter_context(tc.tile_pool(name="results", bufs=8))
        psum = ctx.enter_context(tc.psum_pool(name="psum", bufs=8))
        ctx.enter_context(tc.manual_schedule())

        adj_view = adjacency.rearrange("(s p n) j -> s p n j", p=P, n=LOAD_TILES)
        out_view = out.rearrange(
            "(s p h n) g -> s h p n g", p=P, h=UNITS_PER_LOAD, n=UNIT_TILES
        )

        x_raw = keep.tile([P, PACK, K], BF16)
        w_raw = keep.tile([P, PACK, K], BF16)
        adj_rows = []
        for s in range(LOADS):
            a_rows = adj.tile([P, LOAD_TILES, K], BF16)
            if s == 0:
                for h in range(UNITS_PER_LOAD):
                    tiles = slice(h * UNIT_TILES, (h + 1) * UNIT_TILES)
                    nc.sync.dma_start(out=a_rows[:, tiles, :], in_=adj_view[s, :, tiles, :])
                nc.sync.dma_start(
                    out=x_raw[:].rearrange("p (u e) f -> p u (e f)", u=2, e=2),
                    in_=x.rearrange("(u p e) f -> p u (e f)", u=2, p=P, e=2),
                )
            else:
                nc.sync.dma_start(out=a_rows[:], in_=adj_view[s])
            if s == 1:
                nc.sync.dma_start(
                    out=w_raw[:], in_=W.rearrange("(t p) g -> p t g", t=PACK, p=P)
                )
            adj_rows.append(a_rows)

        ident_bf16 = keep.tile([P, P], BF16)
        make_identity(nc, ident_bf16[:])
        identity = keep.tile([P, P], F32)
        make_identity(nc, identity[:])

        x_grouped = keep.tile([P, K, PACK], BF16, align_bytes=64)
        x_codes = keep.tile([P, K], U32, align_bytes=64)
        x_scales = keep.tile([P, K], U8, align_bytes=64)
        w_grouped = keep.tile([P, K, PACK], BF16, align_bytes=64)
        w_codes = keep.tile([P, K], U32, align_bytes=64)
        w_scales = keep.tile([P, K], U8, align_bytes=64)

        def group_x(engine_copy, first, last):
            engine_copy(
                out=x_grouped[:, first:last, :].rearrange("p (f i) t -> p f t i", i=PACK),
                in_=x_raw[:, :, first:last].rearrange("p t (f i) -> p f t i", i=PACK),
            )

        def quantise_x():
            nc.vector.quantize_mx(
                out=x_codes[:].bitcast(FP8X4),
                scales=x_scales[:],
                in_=x_grouped[:].rearrange("p f t -> p (f t)"),
            )

        def gpsimd_copy(out, in_):
            nc.gpsimd.tensor_scalar(
                out=out, in0=in_, scalar1=1.0, scalar2=0.0, op0=MULT, op1=ADD
            )

        def group_w(engine_copy, quarter):
            cols = slice(quarter * P, (quarter + 1) * P)
            engine_copy(
                out=w_grouped[:, cols, :].rearrange("p (g i) t -> p g t i", i=PACK),
                in_=w_raw[:, :, cols].rearrange("p t (g i) -> p g t i", i=PACK),
            )

        def quantise_w():
            nc.vector.quantize_mx(
                out=w_codes[:].bitcast(FP8X4),
                scales=w_scales[:],
                in_=w_grouped[:].rearrange("p g t -> p (g t)"),
            )

        norm_rows, degrees, inverses, turned, folded = {}, {}, {}, {}, {}
        adj_grouped, adj_codes, adj_scales = {}, {}, {}
        pooled_banks, pooled_grouped, pooled_codes, pooled_scales = {}, {}, {}, {}
        out_banks, out_rows = {}, {}

        def new_bank():
            bank = psum.tile([P, K], F32, name="bank")
            return bank

        def unit_rows(k, n):
            return adj_rows[k // UNITS_PER_LOAD][:, (k % UNITS_PER_LOAD) * UNIT_TILES + n, :]

        def keep_busy(count, k, n):
            bank = new_bank()
            for repeat in range(count):
                nc.tensor.matmul(
                    out=bank[:], lhsT=ident_bf16[:], rhs=unit_rows(k, n), start=True, stop=True
                )

        def fold_rows(k):
            bank = new_bank()[:, : UNIT_TILES * SUM_COLS].rearrange(
                "p (n w) -> p n w", n=UNIT_TILES
            )
            blocks = K // SUM_COLS
            for n in range(UNIT_TILES):
                if not tensor_sums(k, n):
                    continue
                for b in range(blocks):
                    nc.tensor.matmul(
                        out=bank[:, n, :],
                        lhsT=ident_bf16[:],
                        rhs=unit_rows(k, n)[:, b * SUM_COLS : (b + 1) * SUM_COLS],
                        start=(b == 0),
                        stop=(b == blocks - 1),
                    )
            folded[k] = bank

        def sum_rows(k, skip=None):
            rows = work.tile([P, UNIT_TILES, K], BF16)
            deg = work.tile([P, UNIT_TILES], F32)
            if all(tensor_sums(k, n) for n in range(UNIT_TILES)):
                nc.vector.tensor_reduce(out=deg[:], in_=folded[k], axis=AXIS_X, op=ADD)
            else:
                for n in range(UNIT_TILES):
                    if n == skip:
                        continue
                    if tensor_sums(k, n):
                        nc.vector.tensor_reduce(
                            out=deg[:, n : n + 1], in_=folded[k][:, n, :], axis=AXIS_X, op=ADD
                        )
                        continue
                    nc.vector.tensor_scalar(
                        out=rows[:, n, :],
                        in0=unit_rows(k, n),
                        scalar1=1.0,
                        scalar2=None,
                        op0=MULT,
                        op1=ADD,
                        accum_out=deg[:, n : n + 1],
                    )
            norm_rows[k], degrees[k] = rows, deg

        def sum_folded(k):
            nc.vector.tensor_reduce(
                out=degrees[k][:, 1:2], in_=folded[k][:, 1, :], axis=AXIS_X, op=ADD
            )

        def scalar_sum(k, n):
            nc.scalar.activation(
                out=norm_rows[k][:, n, :],
                in_=unit_rows(k, n),
                func=COPY,
                accum_out=degrees[k][:, n : n + 1],
            )

        def invert_sums(k):
            inv = work.tile([P, UNIT_TILES], F32)
            nc.vector.reciprocal(out=inv[:], in_=degrees[k][:])
            inverses[k] = inv

        def scale_rows(k):
            for n in range(UNIT_TILES):
                if not gpsimd_scale(k, n):
                    nc.vector.tensor_scalar(
                        out=norm_rows[k][:, n, :],
                        in0=unit_rows(k, n),
                        scalar1=inverses[k][:, n : n + 1],
                        scalar2=None,
                        op0=MULT,
                    )

        def scale_rows_gpsimd(k):
            for n in range(UNIT_TILES):
                if gpsimd_scale(k, n):
                    nc.gpsimd.tensor_scalar(
                        out=norm_rows[k][:, n, :],
                        in0=unit_rows(k, n),
                        scalar1=inverses[k][:, n : n + 1],
                        scalar2=0.0,
                        op0=MULT,
                        op1=ADD,
                    )

        def transpose_rows(k):
            words = norm_rows[k][:].bitcast(F32)
            bank = new_bank()[:].rearrange("p (n u i) -> p n u i", n=UNIT_TILES, u=2)
            for n in range(UNIT_TILES):
                for u in range(2):
                    nc.tensor.transpose(
                        out=bank[:, n, u, :],
                        in_=words[:, n, u * P : (u + 1) * P],
                        identity=identity[:],
                    )
            turned[k] = bank

        def gather_words(k):
            grouped = work.tile([P, UNIT_COLS, PACK], BF16, align_bytes=64)
            copy = nc.scalar.copy if k in SCALAR_GATHERS else nc.vector.tensor_copy
            copy(
                out=grouped[:].bitcast(F32).rearrange("p (n i) u -> p n i u", n=UNIT_TILES),
                in_=turned[k].rearrange("p n u i -> p n i u"),
            )
            adj_grouped[k] = grouped

        def quantise_adj(k):
            codes = work.tile([P, UNIT_COLS], U32, align_bytes=64)
            scales = work.tile([P, UNIT_COLS], U8, align_bytes=64)
            nc.vector.quantize_mx(
                out=codes[:].bitcast(FP8X4),
                scales=scales[:],
                in_=adj_grouped[k][:].rearrange("p c t -> p (c t)"),
            )
            adj_codes[k], adj_scales[k] = codes, scales

        def pool_features(k):
            for n in range(UNIT_TILES):
                cols = slice(n * P, (n + 1) * P)
                bank = new_bank()[:].rearrange("p (t i) -> p t i", t=PACK)
                for t in range(PACK):
                    feats = slice(t * P, (t + 1) * P)
                    nc.tensor.matmul_mx(
                        out=bank[:, t, :],
                        lhsT=x_codes[:, feats].bitcast(FP8X4),
                        lhsT_scale=x_scales[:, feats],
                        rhs=adj_codes[k][:, cols].bitcast(FP8X4),
                        rhs_scale=adj_scales[k][:, cols],
                        start=True,
                        stop=True,
                    )
                pooled_banks[k, n] = bank

        def regroup_pooled(k):
            grouped2 = work.tile([P, UNIT_COLS, PACK], BF16, align_bytes=64)
            for n in range(UNIT_TILES):
                dst = grouped2[:, n * P : (n + 1) * P, :]
                src = pooled_banks[k, n].rearrange("p t i -> p i t")
                if vector_regroup(k, n):
                    nc.vector.tensor_copy(out=dst, in_=src)
                else:
                    nc.scalar.copy(out=dst, in_=src)
            pooled_grouped[k] = grouped2

        def quantise_pooled(k):
            codes2 = work.tile([P, UNIT_COLS], U32, align_bytes=64)
            scales2 = work.tile([P, UNIT_COLS], U8, align_bytes=64)
            nc.vector.quantize_mx(
                out=codes2[:].bitcast(FP8X4),
                scales=scales2[:],
                in_=pooled_grouped[k][:].rearrange("p c t -> p (c t)"),
            )
            pooled_codes[k], pooled_scales[k] = codes2, scales2

        def project(k):
            for n in range(UNIT_TILES):
                cols = slice(n * P, (n + 1) * P)
                acc = new_bank()
                nc.tensor.matmul_mx(
                    out=acc[:],
                    lhsT=pooled_codes[k][:, cols].bitcast(FP8X4),
                    lhsT_scale=pooled_scales[k][:, cols],
                    rhs=w_codes[:].bitcast(FP8X4),
                    rhs_scale=w_scales[:],
                    start=True,
                    stop=True,
                )
                out_banks[k, n] = acc

        def relu_scalar(k):
            result = results.tile([P, UNIT_TILES, K], F32)
            for n in range(UNIT_TILES):
                if not vector_relu(k, n):
                    nc.scalar.activation(out=result[:, n, :], in_=out_banks[k, n][:], func=RELU)
            out_rows[k] = result

        def relu_vector(k):
            for n in range(UNIT_TILES):
                if vector_relu(k, n):
                    nc.vector.tensor_scalar(
                        out=out_rows[k][:, n, :],
                        in0=out_banks[k, n][:],
                        scalar1=0.0,
                        scalar2=None,
                        op0=MAX,
                    )

        def store(k):
            result = out_rows[k]
            rows = out_view[k // UNITS_PER_LOAD, k % UNITS_PER_LOAD]
            if k >= UNITS - 3:
                for n in range(UNIT_TILES):
                    nc.sync.dma_start(out=rows[:, n, :], in_=result[:, n, :])
            else:
                nc.sync.dma_start(out=rows, in_=result[:])

        done = set()

        def run(stage, k):
            if 0 <= k < UNITS and (stage, k) not in done:
                done.add((stage, k))
                stage(k)

        keep_busy(4, 0, 0)
        sum_rows(0, skip=1)
        done.add((sum_rows, 0))
        scalar_sum(0, 1)
        run(sum_rows, 1)
        run(invert_sums, 0)
        run(scale_rows, 0)
        run(invert_sums, 1)
        run(transpose_rows, 0)
        group_x(nc.scalar.copy, 256, K)
        group_x(nc.vector.tensor_copy, 0, 128)
        run(scale_rows, 1)
        run(transpose_rows, 1)
        group_x(nc.vector.tensor_copy, 128, 256)
        run(gather_words, 0)
        run(gather_words, 1)
        quantise_x()
        run(fold_rows, 2)
        run(fold_rows, 3)
        run(quantise_adj, 0)
        run(sum_rows, 2)
        run(quantise_adj, 1)
        run(pool_features, 0)
        group_w(gpsimd_copy, 0)
        group_w(nc.scalar.copy, 1)
        run(regroup_pooled, 0)
        run(pool_features, 1)
        run(regroup_pooled, 1)
        run(sum_rows, 3)
        run(invert_sums, 2)
        group_w(nc.vector.tensor_copy, 2)
        run(invert_sums, 3)
        group_w(nc.vector.tensor_copy, 3)
        run(scale_rows, 2)
        run(scale_rows, 3)
        run(transpose_rows, 2)
        run(transpose_rows, 3)
        run(fold_rows, 4)
        run(fold_rows, 5)
        quantise_w()
        run(quantise_pooled, 0)
        sum_rows(4, skip=1)
        done.add((sum_rows, 4))
        run(gather_words, 2)
        run(gather_words, 3)
        run(quantise_adj, 2)
        sum_folded(4)
        run(quantise_pooled, 1)
        run(quantise_adj, 3)
        run(invert_sums, 4)
        run(project, 0)
        run(pool_features, 2)
        run(relu_scalar, 0)
        for step in range(4, UNITS):
            run(invert_sums, step)
            run(scale_rows_gpsimd, step)
            run(project, step - PROJECT_LAG)
            run(relu_scalar, step - PROJECT_LAG)
            run(pool_features, step - POOL_LAG)
            run(regroup_pooled, step - POOL_LAG)
            run(sum_rows, step + 1)
            run(fold_rows, step + 2)
            run(transpose_rows, step - 1)
            run(gather_words, step - GATHER_LAG)
            run(relu_vector, step - PROJECT_LAG)
            run(store, step - PROJECT_LAG)
            run(quantise_pooled, step - REQUANT_LAG)
            run(scale_rows, step)
            run(invert_sums, step + 1)
            run(scale_rows_gpsimd, step + 1)
            run(quantise_adj, step - GATHER_LAG)

        last = UNITS - 1
        run(project, last - 4)
        run(relu_scalar, last - 4)
        run(pool_features, last - 2)
        run(transpose_rows, last)
        run(gather_words, last - 1)
        run(relu_vector, last - 4)
        run(store, last - 4)
        run(quantise_pooled, last - 3)
        run(quantise_adj, last - 1)
        run(gather_words, last)
        run(regroup_pooled, last - 2)
        run(project, last - 3)
        run(relu_scalar, last - 3)
        run(quantise_adj, last)
        run(pool_features, last - 1)
        run(quantise_pooled, last - 2)
        run(relu_vector, last - 3)
        run(store, last - 3)
        run(regroup_pooled, last - 1)
        run(pool_features, last)
        run(project, last - 2)
        run(quantise_pooled, last - 1)
        run(regroup_pooled, last)
        run(relu_scalar, last - 2)
        run(relu_vector, last - 2)
        run(store, last - 2)
        run(project, last - 1)
        run(quantise_pooled, last)
        run(relu_scalar, last - 1)
        run(relu_vector, last - 1)
        run(store, last - 1)
        run(project, last)
        run(relu_scalar, last)
        run(relu_vector, last)
        run(store, last)
